import numpy as np
import ml_dtypes

BF16 = ml_dtypes.bfloat16


def bf(x):
    return np.asarray(x, np.float32).astype(BF16)


def f32(x):
    return np.asarray(x, np.float32)


def f64(x):
    return np.asarray(x).astype(np.float64)


def striped(idx):
    return np.tile(idx.reshape(-1, 16).T, (8, 1))


S, E, P, M, N = 256, 128, 128, 256, 128


def setup_inputs():
    return {
        "table": bf(np.random.standard_normal((S, E))),
        "w_int": bf(np.random.standard_normal((E, M)) / np.sqrt(E)),
        "pat": bf(np.random.standard_normal((P, N))),
        "w_pat": bf(np.random.standard_normal((P, M)) / np.sqrt(P)),
        "b": f32(0.1 * np.random.standard_normal((M, 1))),
        "elapsed": f32(np.random.standard_normal((1, N))),
        "time_w": f32(np.random.standard_normal((M, 1))),
        "time_b": f32(0.1 * np.random.standard_normal((M, 1))),
        "pos": f32(np.arange(N)[None, :] / N),
        "pos_w": f32(np.random.standard_normal((M, 1))),
        "offs": striped(np.random.permutation(np.tile(np.arange(S), 2))[:N]),
    }


def reference(table, w_int, pat, w_pat, b, elapsed, time_w, time_b, pos, pos_w, offs):
    idx = offs[:16].T.reshape(-1)
    x = f64(w_int).T @ f64(table)[idx].T + f64(w_pat).T @ f64(pat) + f64(b)
    return x + np.tanh(f64(time_w) * f64(elapsed) + f64(time_b)) + f64(pos_w) * f64(pos)

@@ -1,0 +1,78 @@
+import concourse.mybir as mybir
+from concourse.masks import make_identity
+
+BF16, F32, U16 = mybir.dt.bfloat16, mybir.dt.float32, mybir.dt.uint16
+TANH = mybir.ActivationFunctionType.Tanh
+ADD = mybir.AluOpType.add
+
+P = 128
+S, E, Q, M, N = 256, 128, 128, 256, 128
+FLOPS = 2 * M * N * (E + Q)
+
+
+def as_row(column):
+    return column.rearrange("n one -> one n")
+
+
+def tile_saintlite_kernel(
+    tc, table, w_int, pat, w_pat, b, elapsed, time_w, time_b, pos, pos_w, offs, out
+):
+    nc = tc.nc
+    with (
+        tc.tile_pool(name="held", bufs=1) as held,
+        tc.psum_pool(name="psum", bufs=1) as psum,
+    ):
+        table_rows = held.tile([P, S // P, E], BF16, name="table_rows")
+        nc.sync.dma_start(table_rows[:], table.rearrange("(h p) e -> p h e", p=P))
+        offsets = held.tile([P, N // 16], U16, name="offsets")
+        nc.sync.dma_start(offsets[:], offs)
+        w_pat_sb = held.tile([Q, M], BF16, name="w_pat_sb")
+        nc.sync.dma_start(w_pat_sb[:], w_pat)
+        pat_sb = held.tile([Q, N], BF16, name="pat_sb")
+        nc.sync.dma_start(pat_sb[:], pat)
+        w_int_sb = held.tile([E, M], BF16, name="w_int_sb")
+        nc.sync.dma_start(w_int_sb[:], w_int)
+
+        angle_weights = held.tile([2, M], F32, name="angle_weights")
+        angle_moving = held.tile([2, N], F32, name="angle_moving")
+        nc.scalar.dma_start(angle_weights[0:1, :], as_row(time_b))
+        nc.scalar.dma_start(angle_weights[1:2, :], as_row(time_w))
+        nc.scalar.dma_start(angle_moving[1:2, :], elapsed)
+        nc.vector.memset(angle_moving[0:1, :], 1.0)
+        ramp_weights = held.tile([2, M], F32, name="ramp_weights")
+        ramp_moving = held.tile([2, N], F32, name="ramp_moving")
+        nc.gpsimd.dma_start(ramp_weights[0:1, :], as_row(b))
+        nc.gpsimd.dma_start(ramp_weights[1:2, :], as_row(pos_w))
+        nc.gpsimd.dma_start(ramp_moving[1:2, :], pos)
+        nc.vector.memset(ramp_moving[0:1, :], 1.0)
+
+        identity = held.tile([P, P], BF16, name="identity")
+        make_identity(nc, identity[:])
+        flipped = psum.tile([E, S], BF16, name="flipped")
+        for h in range(S // P):
+            nc.tensor.transpose(flipped[:, h * P : (h + 1) * P], table_rows[:, h, :], identity[:])
+        window = held.tile([E, S], BF16, name="window")
+        nc.vector.tensor_copy(window[:], flipped[:])
+
+        angle = psum.tile([P, M // P, N], F32, name="angle")
+        for h in range(M // P):
+            nc.tensor.matmul(
+                angle[:, h, :], angle_weights[:, h * P : (h + 1) * P], angle_moving[:], start=True, stop=True
+            )
+        wave = held.tile([P, M // P, N], F32, name="wave")
+        nc.scalar.activation(wave[:], angle[:], TANH)
+
+        sums = [psum.tile([P, N], F32, name=f"sum{h}") for h in range(M // P)]
+        for h in range(M // P):
+            block = slice(h * P, (h + 1) * P)
+            nc.tensor.matmul(sums[h][:], w_pat_sb[:, block], pat_sb[:], start=True, stop=False)
+            nc.tensor.matmul(sums[h][:], ramp_weights[:, block], ramp_moving[:], start=False, stop=False)
+        for h in range(M // P):
+            block = slice(h * P, (h + 1) * P)
+            nc.tensor.matmul(
+                sums[h][:], w_int_sb[:, block], window[:].indirect(offsets[:]), start=False, stop=True
+            )
+            result = held.tile([P, N], F32, name=f"result{h}")
+            nc.vector.tensor_tensor(result[:], sums[h][:], wave[:, h, :], ADD)
+            store_queue = nc.sync if h == 0 else nc.scalar
+            store_queue.dma_start(out[block, :], result[:])

@@ -41,9 +41,9 @@ def tile_saintlite_kernel(
         nc.vector.memset(angle_moving[0:1, :], 1.0)
         ramp_weights = held.tile([2, M], F32, name="ramp_weights")
         ramp_moving = held.tile([2, N], F32, name="ramp_moving")
-        nc.gpsimd.dma_start(ramp_weights[0:1, :], as_row(b))
-        nc.gpsimd.dma_start(ramp_weights[1:2, :], as_row(pos_w))
-        nc.gpsimd.dma_start(ramp_moving[1:2, :], pos)
+        nc.scalar.dma_start(ramp_weights[0:1, :], as_row(b))
+        nc.scalar.dma_start(ramp_weights[1:2, :], as_row(pos_w))
+        nc.scalar.dma_start(ramp_moving[1:2, :], pos)
         nc.vector.memset(ramp_moving[0:1, :], 1.0)
 
         identity = held.tile([P, P], BF16, name="identity")

@@ -3,15 +3,12 @@ from concourse.masks import make_identity
 
 BF16, F32, U16 = mybir.dt.bfloat16, mybir.dt.float32, mybir.dt.uint16
 TANH = mybir.ActivationFunctionType.Tanh
-ADD = mybir.AluOpType.add
+ADD, MULT = mybir.AluOpType.add, mybir.AluOpType.mult
 
 P = 128
 S, E, Q, M, N = 256, 128, 128, 256, 128
+T = M // P
 FLOPS = 2 * M * N * (E + Q)
-
-
-def as_row(column):
-    return column.rearrange("n one -> one n")
 
 
 def tile_saintlite_kernel(
@@ -33,18 +30,23 @@ def tile_saintlite_kernel(
         w_int_sb = held.tile([E, M], BF16, name="w_int_sb")
         nc.sync.dma_start(w_int_sb[:], w_int)
 
-        angle_weights = held.tile([2, M], F32, name="angle_weights")
-        angle_moving = held.tile([2, N], F32, name="angle_moving")
-        nc.scalar.dma_start(angle_weights[0:1, :], as_row(time_b))
-        nc.scalar.dma_start(angle_weights[1:2, :], as_row(time_w))
-        nc.scalar.dma_start(angle_moving[1:2, :], elapsed)
-        nc.vector.memset(angle_moving[0:1, :], 1.0)
-        ramp_weights = held.tile([2, M], F32, name="ramp_weights")
-        ramp_moving = held.tile([2, N], F32, name="ramp_moving")
-        nc.scalar.dma_start(ramp_weights[0:1, :], as_row(b))
-        nc.scalar.dma_start(ramp_weights[1:2, :], as_row(pos_w))
-        nc.scalar.dma_start(ramp_moving[1:2, :], pos)
-        nc.vector.memset(ramp_moving[0:1, :], 1.0)
+        def load_steps(queue, row, name):
+            repeated = held.tile([P, N], F32, name=name)
+            queue.dma_start(repeated[:], row.rearrange("one n -> (one n)").partition_broadcast(P))
+            return repeated
+
+        def load_features(queue, column, name):
+            halves = held.tile([P, T], F32, name=name)
+            with nc.allow_non_contiguous_dma(reason="one float32 for each partition and half"):
+                queue.dma_start(halves[:], column.rearrange("(t p) one -> p (t one)", t=T))
+            return halves
+
+        elapsed_sb = load_steps(nc.scalar, elapsed, "elapsed_sb")
+        time_w_sb = load_features(nc.scalar, time_w, "time_w_sb")
+        time_b_sb = load_features(nc.scalar, time_b, "time_b_sb")
+        pos_sb = load_steps(nc.scalar, pos, "pos_sb")
+        pos_w_sb = load_features(nc.scalar, pos_w, "pos_w_sb")
+        b_sb = load_features(nc.sync, b, "b_sb")
 
         identity = held.tile([P, P], BF16, name="identity")
         make_identity(nc, identity[:])
@@ -54,25 +56,29 @@ def tile_saintlite_kernel(
         window = held.tile([E, S], BF16, name="window")
         nc.vector.tensor_copy(window[:], flipped[:])
 
-        angle = psum.tile([P, M // P, N], F32, name="angle")
-        for h in range(M // P):
-            nc.tensor.matmul(
-                angle[:, h, :], angle_weights[:, h * P : (h + 1) * P], angle_moving[:], start=True, stop=True
-            )
-        wave = held.tile([P, M // P, N], F32, name="wave")
-        nc.scalar.activation(wave[:], angle[:], TANH)
+        w_pat_halves = w_pat_sb[:].rearrange("q (t p) -> q t p", t=T)
+        w_int_halves = w_int_sb[:].rearrange("e (t p) -> e t p", t=T)
+        out_halves = out.rearrange("(t p) j -> p t j", t=T)
 
-        sums = [psum.tile([P, N], F32, name=f"sum{h}") for h in range(M // P)]
-        for h in range(M // P):
-            block = slice(h * P, (h + 1) * P)
-            nc.tensor.matmul(sums[h][:], w_pat_sb[:, block], pat_sb[:], start=True, stop=False)
-            nc.tensor.matmul(sums[h][:], ramp_weights[:, block], ramp_moving[:], start=False, stop=False)
-        for h in range(M // P):
-            block = slice(h * P, (h + 1) * P)
-            nc.tensor.matmul(
-                sums[h][:], w_int_sb[:, block], window[:].indirect(offsets[:]), start=False, stop=True
+        sums = [psum.tile([P, N], F32, name=f"sum{t}") for t in range(T)]
+        rest = held.tile([P, T, N], F32, name="rest")
+        for t in range(T):
+            nc.tensor.matmul(sums[t][:], w_pat_halves[:, t, :], pat_sb[:], start=True, stop=False)
+            wave = held.tile([P, N], F32, name=f"wave{t}")
+            nc.scalar.activation(
+                wave[:], elapsed_sb[:], TANH, bias=time_b_sb[:, t : t + 1], scale=time_w_sb[:, t : t + 1]
             )
-            result = held.tile([P, N], F32, name=f"result{h}")
-            nc.vector.tensor_tensor(result[:], sums[h][:], wave[:, h, :], ADD)
-            store_queue = nc.sync if h == 0 else nc.scalar
-            store_queue.dma_start(out[block, :], result[:])
+            nc.vector.scalar_tensor_tensor(
+                rest[:, t, :], pos_sb[:], pos_w_sb[:, t : t + 1], wave[:], op0=MULT, op1=ADD
+            )
+
+        for t in range(T):
+            nc.tensor.matmul(
+                sums[t][:], w_int_halves[:, t, :], window[:].indirect(offsets[:]), start=False, stop=True
+            )
+            result = held.tile([P, N], F32, name=f"result{t}")
+            nc.vector.scalar_tensor_tensor(
+                result[:], sums[t][:], b_sb[:, t : t + 1], rest[:, t, :], op0=ADD, op1=ADD
+            )
+            store_queue = nc.sync if t == 0 else nc.scalar
+            store_queue.dma_start(out_halves[:, t, :], result[:])

@@ -35,18 +35,21 @@ def tile_saintlite_kernel(
             queue.dma_start(repeated[:], row.rearrange("one n -> (one n)").partition_broadcast(P))
             return repeated
 
-        def load_features(queue, column, name):
-            halves = held.tile([P, T], F32, name=name)
-            with nc.allow_non_contiguous_dma(reason="one float32 for each partition and half"):
-                queue.dma_start(halves[:], column.rearrange("(t p) one -> p (t one)", t=T))
-            return halves
-
+        feature_vectors = (time_w, time_b, pos_w, b)
+        V = len(feature_vectors)
+        feature_rows = held.tile([V * T, P], F32, name="feature_rows")
+        for v, column in enumerate(feature_vectors):
+            nc.scalar.dma_start(feature_rows[v * T : (v + 1) * T, :], column.rearrange("(t p) one -> t (p one)", t=T))
         elapsed_sb = load_steps(nc.scalar, elapsed, "elapsed_sb")
-        time_w_sb = load_features(nc.scalar, time_w, "time_w_sb")
-        time_b_sb = load_features(nc.scalar, time_b, "time_b_sb")
         pos_sb = load_steps(nc.scalar, pos, "pos_sb")
-        pos_w_sb = load_features(nc.scalar, pos_w, "pos_w_sb")
-        b_sb = load_features(nc.sync, b, "b_sb")
+
+        small_identity = held.tile([V * T, V * T], F32, name="small_identity")
+        make_identity(nc, small_identity[:])
+        spread = psum.tile([P, V * T], F32, name="spread")
+        nc.tensor.matmul(spread[:], feature_rows[:], small_identity[:], start=True, stop=True)
+        feature_cols = held.tile([P, V, T], F32, name="feature_cols")
+        nc.vector.tensor_copy(feature_cols[:].rearrange("p v t -> p (v t)"), spread[:])
+        time_w_sb, time_b_sb, pos_w_sb, b_sb = (feature_cols[:, v, :] for v in range(V))
 
         identity = held.tile([P, P], BF16, name="identity")
         make_identity(nc, identity[:])

@@ -30,18 +30,21 @@ def tile_saintlite_kernel(
         w_int_sb = held.tile([E, M], BF16, name="w_int_sb")
         nc.sync.dma_start(w_int_sb[:], w_int)
 
-        def load_steps(queue, row, name):
-            repeated = held.tile([P, N], F32, name=name)
-            queue.dma_start(repeated[:], row.rearrange("one n -> (one n)").partition_broadcast(P))
-            return repeated
-
         feature_vectors = (time_w, time_b, pos_w, b)
         V = len(feature_vectors)
         feature_rows = held.tile([V * T, P], F32, name="feature_rows")
         for v, column in enumerate(feature_vectors):
             nc.scalar.dma_start(feature_rows[v * T : (v + 1) * T, :], column.rearrange("(t p) one -> t (p one)", t=T))
-        elapsed_sb = load_steps(nc.scalar, elapsed, "elapsed_sb")
-        pos_sb = load_steps(nc.scalar, pos, "pos_sb")
+        elapsed_row = held.tile([1, N], F32, name="elapsed_row")
+        nc.scalar.dma_start(elapsed_row[:], elapsed)
+        pos_row = held.tile([1, N], F32, name="pos_row")
+        nc.scalar.dma_start(pos_row[:], pos)
+        ones_row = held.tile([1, P], F32, name="ones_row")
+        nc.vector.memset(ones_row[:], 1.0)
+        elapsed_all = psum.tile([P, N], F32, name="elapsed_all")
+        nc.tensor.matmul(elapsed_all[:], ones_row[:], elapsed_row[:], start=True, stop=True)
+        pos_all = psum.tile([P, N], F32, name="pos_all")
+        nc.tensor.matmul(pos_all[:], ones_row[:], pos_row[:], start=True, stop=True)
 
         small_identity = held.tile([V * T, V * T], F32, name="small_identity")
         make_identity(nc, small_identity[:])
@@ -69,10 +72,10 @@ def tile_saintlite_kernel(
             nc.tensor.matmul(sums[t][:], w_pat_halves[:, t, :], pat_sb[:], start=True, stop=False)
             wave = held.tile([P, N], F32, name=f"wave{t}")
             nc.scalar.activation(
-                wave[:], elapsed_sb[:], TANH, bias=time_b_sb[:, t : t + 1], scale=time_w_sb[:, t : t + 1]
+                wave[:], elapsed_all[:], TANH, bias=time_b_sb[:, t : t + 1], scale=time_w_sb[:, t : t + 1]
             )
             nc.vector.scalar_tensor_tensor(
-                rest[:, t, :], pos_sb[:], pos_w_sb[:, t : t + 1], wave[:], op0=MULT, op1=ADD
+                rest[:, t, :], pos_all[:], pos_w_sb[:, t : t + 1], wave[:], op0=MULT, op1=ADD
             )
 
         for t in range(T):

@@ -9,6 +9,8 @@ P = 128
 S, E, Q, M, N = 256, 128, 128, 256, 128
 T = M // P
 FLOPS = 2 * M * N * (E + Q)
+WARM_COLUMNS = 512
+WARM_MATMULS = 4
 
 
 def tile_saintlite_kernel(
@@ -19,6 +21,12 @@ def tile_saintlite_kernel(
         tc.tile_pool(name="held", bufs=1) as held,
         tc.psum_pool(name="psum", bufs=1) as psum,
     ):
+        zeros = held.tile([P, WARM_COLUMNS], BF16, name="zeros")
+        nc.vector.memset(zeros[:], 0.0)
+        unread = psum.tile([P, WARM_COLUMNS], F32, name="unread")
+        for i in range(WARM_MATMULS):
+            nc.tensor.matmul(unread[:], zeros[:, 0:P], zeros[:], start=True, stop=True)
+
         table_rows = held.tile([P, S // P, E], BF16, name="table_rows")
         nc.sync.dma_start(table_rows[:], table.rearrange("(h p) e -> p h e", p=P))
         offsets = held.tile([P, N // 16], U16, name="offsets")

@@ -3,7 +3,7 @@ from concourse.masks import make_identity
 
 BF16, F32, U16 = mybir.dt.bfloat16, mybir.dt.float32, mybir.dt.uint16
 TANH = mybir.ActivationFunctionType.Tanh
-ADD, MULT = mybir.AluOpType.add, mybir.AluOpType.mult
+ADD = mybir.AluOpType.add
 
 P = 128
 S, E, Q, M, N = 256, 128, 128, 256, 128
@@ -11,6 +11,10 @@ T = M // P
 FLOPS = 2 * M * N * (E + Q)
 WARM_COLUMNS = 512
 WARM_MATMULS = 4
+
+
+def as_row(column):
+    return column.rearrange("n one -> one n")
 
 
 def tile_saintlite_kernel(
@@ -28,39 +32,28 @@ def tile_saintlite_kernel(
             nc.tensor.matmul(unread[:], zeros[:, 0:P], zeros[:], start=True, stop=True)
 
         table_rows = held.tile([P, S // P, E], BF16, name="table_rows")
-        nc.sync.dma_start(table_rows[:], table.rearrange("(h p) e -> p h e", p=P))
         offsets = held.tile([P, N // 16], U16, name="offsets")
-        nc.sync.dma_start(offsets[:], offs)
         w_pat_sb = held.tile([Q, M], BF16, name="w_pat_sb")
-        nc.sync.dma_start(w_pat_sb[:], w_pat)
         pat_sb = held.tile([Q, N], BF16, name="pat_sb")
-        nc.sync.dma_start(pat_sb[:], pat)
         w_int_sb = held.tile([E, M], BF16, name="w_int_sb")
+        angle_weights = held.tile([2, M], F32, name="angle_weights")
+        angle_moving = held.tile([2, N], F32, name="angle_moving")
+        ramp_weights = held.tile([2, M], F32, name="ramp_weights")
+        ramp_moving = held.tile([2, N], F32, name="ramp_moving")
+        nc.vector.memset(angle_moving[0:1, :], 1.0)
+        nc.vector.memset(ramp_moving[0:1, :], 1.0)
+
+        nc.sync.dma_start(table_rows[:], table.rearrange("(h p) e -> p h e", p=P))
+        nc.scalar.dma_start(angle_weights[0:1, :], as_row(time_b))
+        nc.sync.dma_start(angle_moving[1:2, :], elapsed)
+        nc.scalar.dma_start(angle_weights[1:2, :], as_row(time_w))
+        nc.sync.dma_start(w_pat_sb[:], w_pat)
+        nc.scalar.dma_start(pat_sb[:], pat)
+        nc.sync.dma_start(ramp_weights[0:1, :], as_row(b))
+        nc.scalar.dma_start(ramp_weights[1:2, :], as_row(pos_w))
+        nc.sync.dma_start(offsets[:], offs)
+        nc.scalar.dma_start(ramp_moving[1:2, :], pos)
         nc.sync.dma_start(w_int_sb[:], w_int)
-
-        feature_vectors = (time_w, time_b, pos_w, b)
-        V = len(feature_vectors)
-        feature_rows = held.tile([V * T, P], F32, name="feature_rows")
-        for v, column in enumerate(feature_vectors):
-            nc.scalar.dma_start(feature_rows[v * T : (v + 1) * T, :], column.rearrange("(t p) one -> t (p one)", t=T))
-        elapsed_row = held.tile([1, N], F32, name="elapsed_row")
-        nc.scalar.dma_start(elapsed_row[:], elapsed)
-        pos_row = held.tile([1, N], F32, name="pos_row")
-        nc.scalar.dma_start(pos_row[:], pos)
-        ones_row = held.tile([1, P], F32, name="ones_row")
-        nc.vector.memset(ones_row[:], 1.0)
-        elapsed_all = psum.tile([P, N], F32, name="elapsed_all")
-        nc.tensor.matmul(elapsed_all[:], ones_row[:], elapsed_row[:], start=True, stop=True)
-        pos_all = psum.tile([P, N], F32, name="pos_all")
-        nc.tensor.matmul(pos_all[:], ones_row[:], pos_row[:], start=True, stop=True)
-
-        small_identity = held.tile([V * T, V * T], F32, name="small_identity")
-        make_identity(nc, small_identity[:])
-        spread = psum.tile([P, V * T], F32, name="spread")
-        nc.tensor.matmul(spread[:], feature_rows[:], small_identity[:], start=True, stop=True)
-        feature_cols = held.tile([P, V, T], F32, name="feature_cols")
-        nc.vector.tensor_copy(feature_cols[:].rearrange("p v t -> p (v t)"), spread[:])
-        time_w_sb, time_b_sb, pos_w_sb, b_sb = (feature_cols[:, v, :] for v in range(V))
 
         identity = held.tile([P, P], BF16, name="identity")
         make_identity(nc, identity[:])
@@ -70,29 +63,25 @@ def tile_saintlite_kernel(
         window = held.tile([E, S], BF16, name="window")
         nc.vector.tensor_copy(window[:], flipped[:])
 
-        w_pat_halves = w_pat_sb[:].rearrange("q (t p) -> q t p", t=T)
-        w_int_halves = w_int_sb[:].rearrange("e (t p) -> e t p", t=T)
-        out_halves = out.rearrange("(t p) j -> p t j", t=T)
-
-        sums = [psum.tile([P, N], F32, name=f"sum{t}") for t in range(T)]
-        rest = held.tile([P, T, N], F32, name="rest")
-        for t in range(T):
-            nc.tensor.matmul(sums[t][:], w_pat_halves[:, t, :], pat_sb[:], start=True, stop=False)
-            wave = held.tile([P, N], F32, name=f"wave{t}")
-            nc.scalar.activation(
-                wave[:], elapsed_all[:], TANH, bias=time_b_sb[:, t : t + 1], scale=time_w_sb[:, t : t + 1]
-            )
-            nc.vector.scalar_tensor_tensor(
-                rest[:, t, :], pos_all[:], pos_w_sb[:, t : t + 1], wave[:], op0=MULT, op1=ADD
-            )
-
+        angle = psum.tile([P, T, N], F32, name="angle")
         for t in range(T):
             nc.tensor.matmul(
-                sums[t][:], w_int_halves[:, t, :], window[:].indirect(offsets[:]), start=False, stop=True
+                angle[:, t, :], angle_weights[:, t * P : (t + 1) * P], angle_moving[:], start=True, stop=True
+            )
+        wave = held.tile([P, T, N], F32, name="wave")
+        nc.scalar.activation(wave[:], angle[:], TANH)
+
+        sums = [psum.tile([P, N], F32, name=f"sum{t}") for t in range(T)]
+        for t in range(T):
+            half = slice(t * P, (t + 1) * P)
+            nc.tensor.matmul(sums[t][:], w_pat_sb[:, half], pat_sb[:], start=True, stop=False)
+            nc.tensor.matmul(sums[t][:], ramp_weights[:, half], ramp_moving[:], start=False, stop=False)
+        for t in range(T):
+            half = slice(t * P, (t + 1) * P)
+            nc.tensor.matmul(
+                sums[t][:], w_int_sb[:, half], window[:].indirect(offsets[:]), start=False, stop=True
             )
             result = held.tile([P, N], F32, name=f"result{t}")
-            nc.vector.scalar_tensor_tensor(
-                result[:], sums[t][:], b_sb[:, t : t + 1], rest[:, t, :], op0=ADD, op1=ADD
-            )
+            nc.vector.tensor_tensor(result[:], sums[t][:], wave[:, t, :], ADD)
             store_queue = nc.sync if t == 0 else nc.scalar
-            store_queue.dma_start(out_halves[:, t, :], result[:])
+            store_queue.dma_start(out[half, :], result[:])

@@ -3,7 +3,7 @@ from concourse.masks import make_identity
 
 BF16, F32, U16 = mybir.dt.bfloat16, mybir.dt.float32, mybir.dt.uint16
 TANH = mybir.ActivationFunctionType.Tanh
-ADD = mybir.AluOpType.add
+ADD, MULT = mybir.AluOpType.add, mybir.AluOpType.mult
 
 P = 128
 S, E, Q, M, N = 256, 128, 128, 256, 128
@@ -11,10 +11,6 @@ T = M // P
 FLOPS = 2 * M * N * (E + Q)
 WARM_COLUMNS = 512
 WARM_MATMULS = 4
-
-
-def as_row(column):
-    return column.rearrange("n one -> one n")
 
 
 def tile_saintlite_kernel(
@@ -32,28 +28,38 @@ def tile_saintlite_kernel(
             nc.tensor.matmul(unread[:], zeros[:, 0:P], zeros[:], start=True, stop=True)
 
         table_rows = held.tile([P, S // P, E], BF16, name="table_rows")
-        offsets = held.tile([P, N // 16], U16, name="offsets")
-        w_pat_sb = held.tile([Q, M], BF16, name="w_pat_sb")
-        pat_sb = held.tile([Q, N], BF16, name="pat_sb")
-        w_int_sb = held.tile([E, M], BF16, name="w_int_sb")
-        angle_weights = held.tile([2, M], F32, name="angle_weights")
-        angle_moving = held.tile([2, N], F32, name="angle_moving")
-        ramp_weights = held.tile([2, M], F32, name="ramp_weights")
-        ramp_moving = held.tile([2, N], F32, name="ramp_moving")
-        nc.vector.memset(angle_moving[0:1, :], 1.0)
-        nc.vector.memset(ramp_moving[0:1, :], 1.0)
-
         nc.sync.dma_start(table_rows[:], table.rearrange("(h p) e -> p h e", p=P))
-        nc.scalar.dma_start(angle_weights[0:1, :], as_row(time_b))
-        nc.sync.dma_start(angle_moving[1:2, :], elapsed)
-        nc.scalar.dma_start(angle_weights[1:2, :], as_row(time_w))
-        nc.sync.dma_start(w_pat_sb[:], w_pat)
-        nc.scalar.dma_start(pat_sb[:], pat)
-        nc.sync.dma_start(ramp_weights[0:1, :], as_row(b))
-        nc.scalar.dma_start(ramp_weights[1:2, :], as_row(pos_w))
+        offsets = held.tile([P, N // 16], U16, name="offsets")
         nc.sync.dma_start(offsets[:], offs)
-        nc.scalar.dma_start(ramp_moving[1:2, :], pos)
+        w_pat_sb = held.tile([Q, M], BF16, name="w_pat_sb")
+        nc.sync.dma_start(w_pat_sb[:], w_pat)
+        pat_sb = held.tile([Q, N], BF16, name="pat_sb")
+        nc.sync.dma_start(pat_sb[:], pat)
+        w_int_sb = held.tile([E, M], BF16, name="w_int_sb")
         nc.sync.dma_start(w_int_sb[:], w_int)
+
+        feature_vectors = (time_w, time_b, pos_w, b)
+        V = len(feature_vectors)
+        feature_rows = held.tile([V * T, P], F32, name="feature_rows")
+        for v, column in enumerate(feature_vectors):
+            nc.scalar.dma_start(feature_rows[v * T : (v + 1) * T, :], column.rearrange("(t p) one -> t (p one)", t=T))
+        identity_f32 = held.tile([P, P], F32, name="identity_f32")
+        make_identity(nc, identity_f32[:])
+        elapsed_col = held.tile([N, 1], F32, name="elapsed_col")
+        nc.scalar.dma_start(elapsed_col[:], elapsed.rearrange("one n -> n one"))
+        pos_col = held.tile([N, 1], F32, name="pos_col")
+        nc.scalar.dma_start(pos_col[:], pos.rearrange("one n -> n one"))
+
+        spread = psum.tile([P, V * T], F32, name="spread")
+        nc.tensor.matmul(spread[:], feature_rows[:], identity_f32[0 : V * T, 0 : V * T], start=True, stop=True)
+        feature_cols = held.tile([P, V, T], F32, name="feature_cols")
+        nc.scalar.copy(feature_cols[:].rearrange("p v t -> p (v t)"), spread[:])
+
+        elapsed_all = psum.tile([P, N], F32, name="elapsed_all")
+        nc.tensor.transpose(elapsed_all[:], elapsed_col[:].to_broadcast([N, P]), identity_f32[:])
+        pos_all = psum.tile([P, N], F32, name="pos_all")
+        nc.tensor.transpose(pos_all[:], pos_col[:].to_broadcast([N, P]), identity_f32[:])
+        time_w_sb, time_b_sb, pos_w_sb, b_sb = (feature_cols[:, v, :] for v in range(V))
 
         identity = held.tile([P, P], BF16, name="identity")
         make_identity(nc, identity[:])
@@ -63,25 +69,29 @@ def tile_saintlite_kernel(
         window = held.tile([E, S], BF16, name="window")
         nc.vector.tensor_copy(window[:], flipped[:])
 
-        angle = psum.tile([P, T, N], F32, name="angle")
-        for t in range(T):
-            nc.tensor.matmul(
-                angle[:, t, :], angle_weights[:, t * P : (t + 1) * P], angle_moving[:], start=True, stop=True
-            )
-        wave = held.tile([P, T, N], F32, name="wave")
-        nc.scalar.activation(wave[:], angle[:], TANH)
+        w_pat_halves = w_pat_sb[:].rearrange("q (t p) -> q t p", t=T)
+        w_int_halves = w_int_sb[:].rearrange("e (t p) -> e t p", t=T)
+        out_halves = out.rearrange("(t p) j -> p t j", t=T)
 
         sums = [psum.tile([P, N], F32, name=f"sum{t}") for t in range(T)]
+        rest = held.tile([P, T, N], F32, name="rest")
         for t in range(T):
-            half = slice(t * P, (t + 1) * P)
-            nc.tensor.matmul(sums[t][:], w_pat_sb[:, half], pat_sb[:], start=True, stop=False)
-            nc.tensor.matmul(sums[t][:], ramp_weights[:, half], ramp_moving[:], start=False, stop=False)
+            nc.tensor.matmul(sums[t][:], w_pat_halves[:, t, :], pat_sb[:], start=True, stop=False)
+            wave = held.tile([P, N], F32, name=f"wave{t}")
+            nc.scalar.activation(
+                wave[:], elapsed_all[:], TANH, bias=time_b_sb[:, t : t + 1], scale=time_w_sb[:, t : t + 1]
+            )
+            nc.vector.scalar_tensor_tensor(
+                rest[:, t, :], pos_all[:], pos_w_sb[:, t : t + 1], wave[:], op0=MULT, op1=ADD
+            )
+
         for t in range(T):
-            half = slice(t * P, (t + 1) * P)
             nc.tensor.matmul(
-                sums[t][:], w_int_sb[:, half], window[:].indirect(offsets[:]), start=False, stop=True
+                sums[t][:], w_int_halves[:, t, :], window[:].indirect(offsets[:]), start=False, stop=True
             )
             result = held.tile([P, N], F32, name=f"result{t}")
-            nc.vector.tensor_tensor(result[:], sums[t][:], wave[:, t, :], ADD)
+            nc.vector.scalar_tensor_tensor(
+                result[:], sums[t][:], b_sb[:, t : t + 1], rest[:, t, :], op0=ADD, op1=ADD
+            )
             store_queue = nc.sync if t == 0 else nc.scalar
-            store_queue.dma_start(out[half, :], result[:])
+            store_queue.dma_start(out_halves[:, t, :], result[:])

@@ -27,28 +27,40 @@ def tile_saintlite_kernel(
         for i in range(WARM_MATMULS):
             nc.tensor.matmul(unread[:], zeros[:, 0:P], zeros[:], start=True, stop=True)
 
+
+        elapsed_col = held.tile([N, 1], F32, name="elapsed_col")
+        nc.scalar.dma_start(elapsed_col[:], elapsed.rearrange("one n -> n one"))
         table_rows = held.tile([P, S // P, E], BF16, name="table_rows")
         nc.sync.dma_start(table_rows[:], table.rearrange("(h p) e -> p h e", p=P))
         offsets = held.tile([P, N // 16], U16, name="offsets")
         nc.sync.dma_start(offsets[:], offs)
+        feature_vectors = (time_w, time_b, pos_w, b)
+        feature_queues = (nc.scalar, nc.scalar, nc.sync, nc.sync)
+        V = len(feature_vectors)
+        feature_rows = held.tile([V * T, P], F32, name="feature_rows")
+        for v in range(V):
+            feature_queues[v].dma_start(
+                feature_rows[v * T : (v + 1) * T, :], feature_vectors[v].rearrange("(t p) one -> t (p one)", t=T)
+            )
+        pos_col = held.tile([N, 1], F32, name="pos_col")
+        nc.scalar.dma_start(pos_col[:], pos.rearrange("one n -> n one"))
+        w_int_sb = held.tile([E, M], BF16, name="w_int_sb")
+        nc.sync.dma_start(w_int_sb[:], w_int)
         w_pat_sb = held.tile([Q, M], BF16, name="w_pat_sb")
         nc.sync.dma_start(w_pat_sb[:], w_pat)
         pat_sb = held.tile([Q, N], BF16, name="pat_sb")
         nc.sync.dma_start(pat_sb[:], pat)
-        w_int_sb = held.tile([E, M], BF16, name="w_int_sb")
-        nc.sync.dma_start(w_int_sb[:], w_int)
 
-        feature_vectors = (time_w, time_b, pos_w, b)
-        V = len(feature_vectors)
-        feature_rows = held.tile([V * T, P], F32, name="feature_rows")
-        for v, column in enumerate(feature_vectors):
-            nc.scalar.dma_start(feature_rows[v * T : (v + 1) * T, :], column.rearrange("(t p) one -> t (p one)", t=T))
         identity_f32 = held.tile([P, P], F32, name="identity_f32")
         make_identity(nc, identity_f32[:])
-        elapsed_col = held.tile([N, 1], F32, name="elapsed_col")
-        nc.scalar.dma_start(elapsed_col[:], elapsed.rearrange("one n -> n one"))
-        pos_col = held.tile([N, 1], F32, name="pos_col")
-        nc.scalar.dma_start(pos_col[:], pos.rearrange("one n -> n one"))
+
+        identity = held.tile([P, P], BF16, name="identity")
+        make_identity(nc, identity[:])
+        flipped = psum.tile([E, S], BF16, name="flipped")
+        for h in range(S // P):
+            nc.tensor.transpose(flipped[:, h * P : (h + 1) * P], table_rows[:, h, :], identity[:])
+        window = held.tile([E, S], BF16, name="window")
+        nc.vector.tensor_copy(window[:], flipped[:])
 
         spread = psum.tile([P, V * T], F32, name="spread")
         nc.tensor.matmul(spread[:], feature_rows[:], identity_f32[0 : V * T, 0 : V * T], start=True, stop=True)
@@ -60,14 +72,6 @@ def tile_saintlite_kernel(
         pos_all = psum.tile([P, N], F32, name="pos_all")
         nc.tensor.transpose(pos_all[:], pos_col[:].to_broadcast([N, P]), identity_f32[:])
         time_w_sb, time_b_sb, pos_w_sb, b_sb = (feature_cols[:, v, :] for v in range(V))
-
-        identity = held.tile([P, P], BF16, name="identity")
-        make_identity(nc, identity[:])
-        flipped = psum.tile([E, S], BF16, name="flipped")
-        for h in range(S // P):
-            nc.tensor.transpose(flipped[:, h * P : (h + 1) * P], table_rows[:, h, :], identity[:])
-        window = held.tile([E, S], BF16, name="window")
-        nc.vector.tensor_copy(window[:], flipped[:])
 
         w_pat_halves = w_pat_sb[:].rearrange("q (t p) -> q t p", t=T)
         w_int_halves = w_int_sb[:].rearrange("e (t p) -> e t p", t=T)

@@ -34,8 +34,8 @@ def tile_saintlite_kernel(
         nc.sync.dma_start(table_rows[:], table.rearrange("(h p) e -> p h e", p=P))
         offsets = held.tile([P, N // 16], U16, name="offsets")
         nc.sync.dma_start(offsets[:], offs)
-        feature_vectors = (time_w, time_b, pos_w, b)
-        feature_queues = (nc.scalar, nc.scalar, nc.sync, nc.sync)
+        feature_vectors = (time_w, time_b, pos_w)
+        feature_queues = (nc.scalar, nc.scalar, nc.sync)
         V = len(feature_vectors)
         feature_rows = held.tile([V * T, P], F32, name="feature_rows")
         for v in range(V):
@@ -50,9 +50,8 @@ def tile_saintlite_kernel(
         nc.sync.dma_start(w_pat_sb[:], w_pat)
         pat_sb = held.tile([Q, N], BF16, name="pat_sb")
         nc.sync.dma_start(pat_sb[:], pat)
-
-        identity_f32 = held.tile([P, P], F32, name="identity_f32")
-        make_identity(nc, identity_f32[:])
+        b_sb = held.tile([P, T], F32, name="b_sb")
+        nc.sync.dma_start(b_sb[:], b.rearrange("(t p) one -> p (t one)", p=P))
 
         identity = held.tile([P, P], BF16, name="identity")
         make_identity(nc, identity[:])
@@ -62,25 +61,29 @@ def tile_saintlite_kernel(
         window = held.tile([E, S], BF16, name="window")
         nc.vector.tensor_copy(window[:], flipped[:])
 
-        spread = psum.tile([P, V * T], F32, name="spread")
-        nc.tensor.matmul(spread[:], feature_rows[:], identity_f32[0 : V * T, 0 : V * T], start=True, stop=True)
-        feature_cols = held.tile([P, V, T], F32, name="feature_cols")
-        nc.scalar.copy(feature_cols[:].rearrange("p v t -> p (v t)"), spread[:])
-
-        elapsed_all = psum.tile([P, N], F32, name="elapsed_all")
-        nc.tensor.transpose(elapsed_all[:], elapsed_col[:].to_broadcast([N, P]), identity_f32[:])
-        pos_all = psum.tile([P, N], F32, name="pos_all")
-        nc.tensor.transpose(pos_all[:], pos_col[:].to_broadcast([N, P]), identity_f32[:])
-        time_w_sb, time_b_sb, pos_w_sb, b_sb = (feature_cols[:, v, :] for v in range(V))
-
         w_pat_halves = w_pat_sb[:].rearrange("q (t p) -> q t p", t=T)
         w_int_halves = w_int_sb[:].rearrange("e (t p) -> e t p", t=T)
         out_halves = out.rearrange("(t p) j -> p t j", t=T)
 
         sums = [psum.tile([P, N], F32, name=f"sum{t}") for t in range(T)]
+        for t in range(T):
+            nc.tensor.matmul(
+                sums[t][:], w_int_halves[:, t, :], window[:].indirect(offsets[:]), start=True, stop=False
+            )
+
+        identity_f32 = held.tile([P, P], F32, name="identity_f32")
+        make_identity(nc, identity_f32[:])
+        spread = psum.tile([P, V * T], F32, name="spread")
+        nc.tensor.matmul(spread[:], feature_rows[:], identity_f32[0 : V * T, 0 : V * T], start=True, stop=True)
+        feature_cols = held.tile([P, V, T], F32, name="feature_cols")
+        nc.scalar.copy(feature_cols[:].rearrange("p v t -> p (v t)"), spread[:])
+        time_w_sb, time_b_sb, pos_w_sb = (feature_cols[:, v, :] for v in range(V))
+        elapsed_all = psum.tile([P, N], F32, name="elapsed_all")
+        nc.tensor.transpose(elapsed_all[:], elapsed_col[:].to_broadcast([N, P]), identity_f32[:])
+        pos_all = psum.tile([P, N], F32, name="pos_all")
+        nc.tensor.transpose(pos_all[:], pos_col[:].to_broadcast([N, P]), identity_f32[:])
         rest = held.tile([P, T, N], F32, name="rest")
         for t in range(T):
-            nc.tensor.matmul(sums[t][:], w_pat_halves[:, t, :], pat_sb[:], start=True, stop=False)
             wave = held.tile([P, N], F32, name=f"wave{t}")
             nc.scalar.activation(
                 wave[:], elapsed_all[:], TANH, bias=time_b_sb[:, t : t + 1], scale=time_w_sb[:, t : t + 1]
@@ -90,9 +93,7 @@ def tile_saintlite_kernel(
             )
 
         for t in range(T):
-            nc.tensor.matmul(
-                sums[t][:], w_int_halves[:, t, :], window[:].indirect(offsets[:]), start=False, stop=True
-            )
+            nc.tensor.matmul(sums[t][:], w_pat_halves[:, t, :], pat_sb[:], start=False, stop=True)
             result = held.tile([P, N], F32, name=f"result{t}")
             nc.vector.scalar_tensor_tensor(
                 result[:], sums[t][:], b_sb[:, t : t + 1], rest[:, t, :], op0=ADD, op1=ADD

@@ -27,31 +27,32 @@ def tile_saintlite_kernel(
         for i in range(WARM_MATMULS):
             nc.tensor.matmul(unread[:], zeros[:, 0:P], zeros[:], start=True, stop=True)
 
+        unread_tanh = held.tile([P, 1], F32, name="unread_tanh")
+        nc.scalar.activation(unread_tanh[:], zeros[:, 0:1], TANH)
 
+
+        pos_w_sb = held.tile([P, T], F32, name="pos_w_sb")
+        nc.scalar.dma_start(pos_w_sb[:], pos_w.rearrange("(t p) one -> p (t one)", p=P))
+        time_w_sb = held.tile([P, T], F32, name="time_w_sb")
+        nc.sync.dma_start(time_w_sb[:], time_w.rearrange("(t p) one -> p (t one)", p=P))
+        time_b_sb = held.tile([P, T], F32, name="time_b_sb")
+        nc.sync.dma_start(time_b_sb[:], time_b.rearrange("(t p) one -> p (t one)", p=P))
         elapsed_col = held.tile([N, 1], F32, name="elapsed_col")
         nc.scalar.dma_start(elapsed_col[:], elapsed.rearrange("one n -> n one"))
         table_rows = held.tile([P, S // P, E], BF16, name="table_rows")
         nc.sync.dma_start(table_rows[:], table.rearrange("(h p) e -> p h e", p=P))
         offsets = held.tile([P, N // 16], U16, name="offsets")
         nc.sync.dma_start(offsets[:], offs)
-        feature_vectors = (time_w, time_b, pos_w)
-        feature_queues = (nc.scalar, nc.scalar, nc.sync)
-        V = len(feature_vectors)
-        feature_rows = held.tile([V * T, P], F32, name="feature_rows")
-        for v in range(V):
-            feature_queues[v].dma_start(
-                feature_rows[v * T : (v + 1) * T, :], feature_vectors[v].rearrange("(t p) one -> t (p one)", t=T)
-            )
         pos_col = held.tile([N, 1], F32, name="pos_col")
         nc.scalar.dma_start(pos_col[:], pos.rearrange("one n -> n one"))
         w_int_sb = held.tile([E, M], BF16, name="w_int_sb")
         nc.sync.dma_start(w_int_sb[:], w_int)
+        b_sb = held.tile([P, T], F32, name="b_sb")
+        nc.sync.dma_start(b_sb[:], b.rearrange("(t p) one -> p (t one)", p=P))
         w_pat_sb = held.tile([Q, M], BF16, name="w_pat_sb")
         nc.sync.dma_start(w_pat_sb[:], w_pat)
         pat_sb = held.tile([Q, N], BF16, name="pat_sb")
         nc.sync.dma_start(pat_sb[:], pat)
-        b_sb = held.tile([P, T], F32, name="b_sb")
-        nc.sync.dma_start(b_sb[:], b.rearrange("(t p) one -> p (t one)", p=P))
 
         identity = held.tile([P, P], BF16, name="identity")
         make_identity(nc, identity[:])
@@ -65,19 +66,8 @@ def tile_saintlite_kernel(
         w_int_halves = w_int_sb[:].rearrange("e (t p) -> e t p", t=T)
         out_halves = out.rearrange("(t p) j -> p t j", t=T)
 
-        sums = [psum.tile([P, N], F32, name=f"sum{t}") for t in range(T)]
-        for t in range(T):
-            nc.tensor.matmul(
-                sums[t][:], w_int_halves[:, t, :], window[:].indirect(offsets[:]), start=True, stop=False
-            )
-
         identity_f32 = held.tile([P, P], F32, name="identity_f32")
         make_identity(nc, identity_f32[:])
-        spread = psum.tile([P, V * T], F32, name="spread")
-        nc.tensor.matmul(spread[:], feature_rows[:], identity_f32[0 : V * T, 0 : V * T], start=True, stop=True)
-        feature_cols = held.tile([P, V, T], F32, name="feature_cols")
-        nc.scalar.copy(feature_cols[:].rearrange("p v t -> p (v t)"), spread[:])
-        time_w_sb, time_b_sb, pos_w_sb = (feature_cols[:, v, :] for v in range(V))
         elapsed_all = psum.tile([P, N], F32, name="elapsed_all")
         nc.tensor.transpose(elapsed_all[:], elapsed_col[:].to_broadcast([N, P]), identity_f32[:])
         pos_all = psum.tile([P, N], F32, name="pos_all")
@@ -90,6 +80,12 @@ def tile_saintlite_kernel(
             )
             nc.vector.scalar_tensor_tensor(
                 rest[:, t, :], pos_all[:], pos_w_sb[:, t : t + 1], wave[:], op0=MULT, op1=ADD
+            )
+
+        sums = [psum.tile([P, N], F32, name=f"sum{t}") for t in range(T)]
+        for t in range(T):
+            nc.tensor.matmul(
+                sums[t][:], w_int_halves[:, t, :], window[:].indirect(offsets[:]), start=True, stop=False
             )
 
         for t in range(T):

@@ -1,7 +1,7 @@
 import concourse.mybir as mybir
 from concourse.masks import make_identity
 
-BF16, F32, U16 = mybir.dt.bfloat16, mybir.dt.float32, mybir.dt.uint16
+BF16, F32, U16, I32 = mybir.dt.bfloat16, mybir.dt.float32, mybir.dt.uint16, mybir.dt.int32
 TANH = mybir.ActivationFunctionType.Tanh
 ADD, MULT = mybir.AluOpType.add, mybir.AluOpType.mult
 
@@ -43,12 +43,10 @@ def tile_saintlite_kernel(
         nc.sync.dma_start(table_rows[:], table.rearrange("(h p) e -> p h e", p=P))
         offsets = held.tile([P, N // 16], U16, name="offsets")
         nc.sync.dma_start(offsets[:], offs)
-        pos_col = held.tile([N, 1], F32, name="pos_col")
-        nc.scalar.dma_start(pos_col[:], pos.rearrange("one n -> n one"))
+        b_sb = held.tile([P, T], F32, name="b_sb")
+        nc.scalar.dma_start(b_sb[:], b.rearrange("(t p) one -> p (t one)", p=P))
         w_int_sb = held.tile([E, M], BF16, name="w_int_sb")
         nc.sync.dma_start(w_int_sb[:], w_int)
-        b_sb = held.tile([P, T], F32, name="b_sb")
-        nc.sync.dma_start(b_sb[:], b.rearrange("(t p) one -> p (t one)", p=P))
         w_pat_sb = held.tile([Q, M], BF16, name="w_pat_sb")
         nc.sync.dma_start(w_pat_sb[:], w_pat)
         pat_sb = held.tile([Q, N], BF16, name="pat_sb")
@@ -70,8 +68,10 @@ def tile_saintlite_kernel(
         make_identity(nc, identity_f32[:])
         elapsed_all = psum.tile([P, N], F32, name="elapsed_all")
         nc.tensor.transpose(elapsed_all[:], elapsed_col[:].to_broadcast([N, P]), identity_f32[:])
-        pos_all = psum.tile([P, N], F32, name="pos_all")
-        nc.tensor.transpose(pos_all[:], pos_col[:].to_broadcast([N, P]), identity_f32[:])
+        step_number = held.tile([P, N], I32, name="step_number")
+        nc.gpsimd.iota(step_number[:], pattern=[[1, N]], base=0, channel_multiplier=0)
+        pos_all = held.tile([P, N], F32, name="pos_all")
+        nc.vector.tensor_scalar_mul(pos_all[:], step_number[:], 1.0 / N)
         rest = held.tile([P, T, N], F32, name="rest")
         for t in range(T):
             wave = held.tile([P, N], F32, name=f"wave{t}")

@@ -31,16 +31,16 @@ def tile_saintlite_kernel(
         nc.scalar.activation(unread_tanh[:], zeros[:, 0:1], TANH)
 
 
-        pos_w_sb = held.tile([P, T], F32, name="pos_w_sb")
-        nc.scalar.dma_start(pos_w_sb[:], pos_w.rearrange("(t p) one -> p (t one)", p=P))
-        time_w_sb = held.tile([P, T], F32, name="time_w_sb")
-        nc.sync.dma_start(time_w_sb[:], time_w.rearrange("(t p) one -> p (t one)", p=P))
-        time_b_sb = held.tile([P, T], F32, name="time_b_sb")
-        nc.sync.dma_start(time_b_sb[:], time_b.rearrange("(t p) one -> p (t one)", p=P))
         elapsed_col = held.tile([N, 1], F32, name="elapsed_col")
         nc.scalar.dma_start(elapsed_col[:], elapsed.rearrange("one n -> n one"))
         table_rows = held.tile([P, S // P, E], BF16, name="table_rows")
         nc.sync.dma_start(table_rows[:], table.rearrange("(h p) e -> p h e", p=P))
+        time_w_sb = held.tile([P, T], F32, name="time_w_sb")
+        nc.sync.dma_start(time_w_sb[:], time_w.rearrange("(t p) one -> p (t one)", p=P))
+        time_b_sb = held.tile([P, T], F32, name="time_b_sb")
+        nc.sync.dma_start(time_b_sb[:], time_b.rearrange("(t p) one -> p (t one)", p=P))
+        pos_w_sb = held.tile([P, T], F32, name="pos_w_sb")
+        nc.scalar.dma_start(pos_w_sb[:], pos_w.rearrange("(t p) one -> p (t one)", p=P))
         offsets = held.tile([P, N // 16], U16, name="offsets")
         nc.sync.dma_start(offsets[:], offs)
         b_sb = held.tile([P, T], F32, name="b_sb")

@@ -27,9 +27,6 @@ def tile_saintlite_kernel(
         for i in range(WARM_MATMULS):
             nc.tensor.matmul(unread[:], zeros[:, 0:P], zeros[:], start=True, stop=True)
 
-        unread_tanh = held.tile([P, 1], F32, name="unread_tanh")
-        nc.scalar.activation(unread_tanh[:], zeros[:, 0:1], TANH)
-
 
         elapsed_col = held.tile([N, 1], F32, name="elapsed_col")
         nc.scalar.dma_start(elapsed_col[:], elapsed.rearrange("one n -> n one"))
@@ -51,6 +48,9 @@ def tile_saintlite_kernel(
         nc.sync.dma_start(w_pat_sb[:], w_pat)
         pat_sb = held.tile([Q, N], BF16, name="pat_sb")
         nc.sync.dma_start(pat_sb[:], pat)
+
+        unread_tanh = held.tile([P, 1], F32, name="unread_tanh")
+        nc.scalar.activation(unread_tanh[:], zeros[:, 0:1], TANH)
 
         identity = held.tile([P, P], BF16, name="identity")
         make_identity(nc, identity[:])

@@ -9,8 +9,6 @@ P = 128
 S, E, Q, M, N = 256, 128, 128, 256, 128
 T = M // P
 FLOPS = 2 * M * N * (E + Q)
-WARM_COLUMNS = 512
-WARM_MATMULS = 4
 
 
 def tile_saintlite_kernel(
@@ -21,12 +19,6 @@ def tile_saintlite_kernel(
         tc.tile_pool(name="held", bufs=1) as held,
         tc.psum_pool(name="psum", bufs=1) as psum,
     ):
-        zeros = held.tile([P, WARM_COLUMNS], BF16, name="zeros")
-        nc.vector.memset(zeros[:], 0.0)
-        unread = psum.tile([P, WARM_COLUMNS], F32, name="unread")
-        for i in range(WARM_MATMULS):
-            nc.tensor.matmul(unread[:], zeros[:, 0:P], zeros[:], start=True, stop=True)
-
 
         elapsed_col = held.tile([N, 1], F32, name="elapsed_col")
         nc.scalar.dma_start(elapsed_col[:], elapsed.rearrange("one n -> n one"))
@@ -49,8 +41,10 @@ def tile_saintlite_kernel(
         pat_sb = held.tile([Q, N], BF16, name="pat_sb")
         nc.sync.dma_start(pat_sb[:], pat)
 
+        zero_column = held.tile([P, 1], F32, name="zero_column")
+        nc.vector.memset(zero_column[:], 0.0)
         unread_tanh = held.tile([P, 1], F32, name="unread_tanh")
-        nc.scalar.activation(unread_tanh[:], zeros[:, 0:1], TANH)
+        nc.scalar.activation(unread_tanh[:], zero_column[:], TANH)
 
         identity = held.tile([P, P], BF16, name="identity")
         make_identity(nc, identity[:])

@@ -88,5 +88,5 @@ def tile_saintlite_kernel(
             nc.vector.scalar_tensor_tensor(
                 result[:], sums[t][:], b_sb[:, t : t + 1], rest[:, t, :], op0=ADD, op1=ADD
             )
-            store_queue = nc.sync if t == 0 else nc.scalar
+            store_queue = nc.scalar if t == 0 else nc.sync
             store_queue.dma_start(out_halves[:, t, :], result[:])

import concourse.mybir as mybir
from concourse.masks import make_identity

BF16, F32, U16, I32 = mybir.dt.bfloat16, mybir.dt.float32, mybir.dt.uint16, mybir.dt.int32
TANH = mybir.ActivationFunctionType.Tanh
ADD, MULT = mybir.AluOpType.add, mybir.AluOpType.mult

P = 128
S, E, Q, M, N = 256, 128, 128, 256, 128
T = M // P
FLOPS = 2 * M * N * (E + Q)


def tile_saintlite_kernel(
    tc, table, w_int, pat, w_pat, b, elapsed, time_w, time_b, pos, pos_w, offs, out
):
    nc = tc.nc
    with (
        tc.tile_pool(name="held", bufs=1) as held,
        tc.psum_pool(name="psum", bufs=1) as psum,
    ):

        elapsed_col = held.tile([N, 1], F32, name="elapsed_col")
        nc.scalar.dma_start(elapsed_col[:], elapsed.rearrange("one n -> n one"))
        table_rows = held.tile([P, S // P, E], BF16, name="table_rows")
        nc.sync.dma_start(table_rows[:], table.rearrange("(h p) e -> p h e", p=P))
        time_w_sb = held.tile([P, T], F32, name="time_w_sb")
        nc.sync.dma_start(time_w_sb[:], time_w.rearrange("(t p) one -> p (t one)", p=P))
        time_b_sb = held.tile([P, T], F32, name="time_b_sb")
        nc.sync.dma_start(time_b_sb[:], time_b.rearrange("(t p) one -> p (t one)", p=P))
        pos_w_sb = held.tile([P, T], F32, name="pos_w_sb")
        nc.scalar.dma_start(pos_w_sb[:], pos_w.rearrange("(t p) one -> p (t one)", p=P))
        offsets = held.tile([P, N // 16], U16, name="offsets")
        nc.sync.dma_start(offsets[:], offs)
        b_sb = held.tile([P, T], F32, name="b_sb")
        nc.scalar.dma_start(b_sb[:], b.rearrange("(t p) one -> p (t one)", p=P))
        w_int_sb = held.tile([E, M], BF16, name="w_int_sb")
        nc.sync.dma_start(w_int_sb[:], w_int)
        w_pat_sb = held.tile([Q, M], BF16, name="w_pat_sb")
        nc.sync.dma_start(w_pat_sb[:], w_pat)
        pat_sb = held.tile([Q, N], BF16, name="pat_sb")
        nc.sync.dma_start(pat_sb[:], pat)

        zero_column = held.tile([P, 1], F32, name="zero_column")
        nc.vector.memset(zero_column[:], 0.0)
        unread_tanh = held.tile([P, 1], F32, name="unread_tanh")
        nc.scalar.activation(unread_tanh[:], zero_column[:], TANH)

        identity = held.tile([P, P], BF16, name="identity")
        make_identity(nc, identity[:])
        flipped = psum.tile([E, S], BF16, name="flipped")
        for h in range(S // P):
            nc.tensor.transpose(flipped[:, h * P : (h + 1) * P], table_rows[:, h, :], identity[:])
        window = held.tile([E, S], BF16, name="window")
        nc.vector.tensor_copy(window[:], flipped[:])

        w_pat_halves = w_pat_sb[:].rearrange("q (t p) -> q t p", t=T)
        w_int_halves = w_int_sb[:].rearrange("e (t p) -> e t p", t=T)
        out_halves = out.rearrange("(t p) j -> p t j", t=T)

        identity_f32 = held.tile([P, P], F32, name="identity_f32")
        make_identity(nc, identity_f32[:])
        elapsed_all = psum.tile([P, N], F32, name="elapsed_all")
        nc.tensor.transpose(elapsed_all[:], elapsed_col[:].to_broadcast([N, P]), identity_f32[:])
        step_number = held.tile([P, N], I32, name="step_number")
        nc.gpsimd.iota(step_number[:], pattern=[[1, N]], base=0, channel_multiplier=0)
        pos_all = held.tile([P, N], F32, name="pos_all")
        nc.vector.tensor_scalar_mul(pos_all[:], step_number[:], 1.0 / N)
        rest = held.tile([P, T, N], F32, name="rest")
        for t in range(T):
            wave = held.tile([P, N], F32, name=f"wave{t}")
            nc.scalar.activation(
                wave[:], elapsed_all[:], TANH, bias=time_b_sb[:, t : t + 1], scale=time_w_sb[:, t : t + 1]
            )
            nc.vector.scalar_tensor_tensor(
                rest[:, t, :], pos_all[:], pos_w_sb[:, t : t + 1], wave[:], op0=MULT, op1=ADD
            )

        sums = [psum.tile([P, N], F32, name=f"sum{t}") for t in range(T)]
        for t in range(T):
            nc.tensor.matmul(
                sums[t][:], w_int_halves[:, t, :], window[:].indirect(offsets[:]), start=True, stop=False
            )

        for t in range(T):
            nc.tensor.matmul(sums[t][:], w_pat_halves[:, t, :], pat_sb[:], start=False, stop=True)
            result = held.tile([P, N], F32, name=f"result{t}")
            nc.vector.scalar_tensor_tensor(
                result[:], sums[t][:], b_sb[:, t : t + 1], rest[:, t, :], op0=ADD, op1=ADD
            )
            store_queue = nc.scalar if t == 0 else nc.sync
            store_queue.dma_start(out_halves[:, t, :], result[:])
